import numpy as np
import ml_dtypes


def mxq(x, axis, fmt="e4m3"):
    dtype, down = {"e4m3": (ml_dtypes.float8_e4m3fn, 7), "e5m2": (ml_dtypes.float8_e5m2, 14)}[fmt]
    v = np.moveaxis(np.asarray(x, np.float32).astype(ml_dtypes.bfloat16).astype(np.float64), axis, -1)
    blocks = v.reshape(v.shape[:-1] + (-1, 32))
    amax = np.abs(blocks).max(-1, keepdims=True)
    byte = np.maximum(np.where(amax > 0, np.frexp(amax)[1] - 1 + 127, 0) - down, 1)
    scale = np.exp2(byte - 127.0)
    codes = (blocks / scale).astype(np.float32).astype(dtype).astype(np.float64)
    return np.moveaxis((codes * scale).reshape(v.shape), -1, axis)


WIDE = False


def mx_kscale(k):
    if not WIDE:
        return np.ones(k)
    levels = np.array([30, -30])
    if k % 512:
        return np.exp2(np.random.permutation(np.resize(levels, k // 32))).repeat(32)
    a = np.empty((k // 512, 16))
    for p in range(k // 512):
        a[p, :8] = np.random.permutation(np.resize(levels, 8))
        for g in range(8):
            far = levels[np.abs(levels - a[p, g]) >= 10]
            a[p, g + 8] = far[np.random.randint(len(far))]
    return np.exp2(a.ravel()).repeat(32)


BF16 = ml_dtypes.bfloat16


def bf(x):
    return np.asarray(x, np.float32).astype(BF16)


def f64(x):
    return np.asarray(x).astype(np.float64)


W, M, K, N = 4, 512, 2048, 1024


def setup_inputs():
    s = mx_kscale(K)
    return {"x": bf(np.random.standard_normal((W, M, K)) * s),
            "weight": bf(np.random.standard_normal((W, N, K)) / np.sqrt(W * K) / s),
            "bias": bf(np.random.standard_normal((W, M, N)) / np.sqrt(W))}


def reference(x, weight, bias):
    w, m, _ = x.shape
    xq = mxq(f64(x), 2, "e5m2")
    wq = mxq(f64(weight), 2, "e4m3")
    y = (xq @ wq.transpose(0, 2, 1)).sum(0) + f64(bias).sum(0)
    m_per_rank = m // w
    return y.reshape(w, m_per_rank, -1)

@@ -1,0 +1,239 @@
+from contextlib import ExitStack
+
+import concourse.mybir as mybir
+from concourse.masks import make_identity
+
+RANKS, M, K, N = 4, 512, 2048, 1024
+FLOPS = 2 * RANKS * M * K * N
+
+F32 = mybir.dt.float32
+BF16 = mybir.dt.bfloat16
+U32 = mybir.dt.uint32
+U8 = mybir.dt.uint8
+E5M2 = mybir.dt.float8_e5m2_x4
+E4M3 = mybir.dt.float8_e4m3fn_x4
+ADD = mybir.AluOpType.add
+
+P = 128
+TILES = 4
+PASSES = K // 512
+WORDS = K // 2
+N_HALF = N // 2
+
+RAW_BUFS = 6
+STAGED_BUFS = 8
+GROUPED_BUFS = 12
+W_CODE_BUFS = 10
+HEAD = (3, 4, 5, 6)
+QFIRST = 0
+
+
+def tile_gemmrstritonpcie_kernel(tc, x, weight, bias, out):
+    nc = tc.nc
+    x_rows = x.rearrange("r (p j) k -> r p j k", j=TILES)
+    w_rows = weight.rearrange("r (h a p j) k -> r h a p j k", h=2, a=2, j=2)
+    bias_rows = bias.rearrange("r (p j) n -> r p j n", j=TILES)
+    out_rows = out.rearrange("r m n -> (r m) n").rearrange("(p j) n -> p j n", j=TILES)
+
+    with ExitStack() as ctx:
+        keep = ctx.enter_context(tc.tile_pool(name="keep", bufs=1))
+        stream = ctx.enter_context(tc.tile_pool(name="stream", bufs=1))
+        psum = ctx.enter_context(tc.psum_pool(name="psum", bufs=1))
+        ctx.enter_context(tc.manual_schedule())
+
+        ident = keep.tile([P, P], F32, name="ident")
+        make_identity(nc, ident[:])
+        bias_sb = [keep.tile([P, TILES, N], BF16, name="bias%d" % r) for r in range(RANKS)]
+        result = {
+            (h, j): keep.tile([P, N_HALF], F32, name="result%d_%d" % (h, j))
+            for h in range(2)
+            for j in range(TILES)
+        }
+
+        raw, staged, grouped, codes, acc = {}, {}, {}, {}, {}
+
+        loads = [("w", 0, 0, 0), ("w", 0, 0, 1)]
+        for r in range(RANKS):
+            for a in range(2):
+                loads.append(("x", 0, r, a))
+                if r + 1 < RANKS:
+                    loads.append(("w", 0, r + 1, a))
+        first_sweep_pairs = list(loads)
+        loads.extend([("w", 1, 0, 0), ("w", 1, 0, 1), ("bias", 0)])
+        for r in range(1, RANKS):
+            loads.extend([("w", 1, r, 0), ("bias", r), ("w", 1, r, 1)])
+        split_pairs = 3
+        state = {"load": 0, "pairs": 0, "reordered": 0}
+
+        def issue_loads():
+            while state["load"] < len(loads):
+                item = loads[state["load"]]
+                if item[0] == "bias":
+                    nc.sync.dma_start(out=bias_sb[item[1]][:], in_=bias_rows[item[1]])
+                else:
+                    if state["pairs"] - RAW_BUFS >= state["reordered"] // 2:
+                        return
+                    kind, h, r, a = item
+                    src = x_rows[r, :, 2 * a : 2 * a + 2, :] if kind == "x" else w_rows[r, h, a]
+                    pair = stream.tile([P, 2, K], BF16, name="raw", tag="raw", bufs=RAW_BUFS)
+                    if state["pairs"] < split_pairs:
+                        for jj in range(2):
+                            nc.sync.dma_start(out=pair[:, jj, :], in_=src[:, jj, :])
+                    else:
+                        nc.sync.dma_start(out=pair[:], in_=src)
+                    for jj in range(2):
+                        raw[(kind, h, r, 2 * a + jj)] = pair[:, jj, :]
+                    state["pairs"] += 1
+                state["load"] += 1
+
+        def reorder(tile, on_scalar):
+            dst = stream.tile([P, 2, WORDS // 2], F32, name="staged", tag="staged", bufs=STAGED_BUFS)
+            src = raw[tile].bitcast(F32).rearrange("p (b u e) -> p u b e", u=2, e=8)
+            view = dst[:].rearrange("p u (b e) -> p u b e", e=8)
+            if on_scalar:
+                nc.scalar.copy(out=view, in_=src)
+            else:
+                nc.vector.tensor_copy(out=view, in_=src)
+            staged[tile] = dst
+            state["reordered"] += 1
+            issue_loads()
+
+        def transpose_bank(kind, h, r, i, s):
+            if kind == "x":
+                parts = [((kind, h, r, i), 2 * s + q) for q in range(2)]
+            else:
+                parts = [((kind, h, r, 2 * i + q), s) for q in range(2)]
+            bank = psum.tile([P, 2, 2, P], F32, name="bank", tag="bank", bufs=4)
+            for q, (tile, g) in enumerate(parts):
+                for u in range(2):
+                    nc.tensor.transpose(bank[:, q, u, :], staged[tile][:, u, P * g : P * (g + 1)], ident[:])
+            dst = stream.tile([P, 2, P, 2], F32, name="grouped", tag="grouped", bufs=GROUPED_BUFS, align_bytes=64)
+            nc.scalar.copy(out=dst[:], in_=bank[:].rearrange("p q u c -> p q c u"))
+            grouped[(kind, h, r, i, s)] = dst
+
+        def quantize(kind, h, r, i, s):
+            if kind == "x":
+                key, cols, fmt = (kind, r, i), slice(256 * s, 256 * (s + 1)), E5M2
+                if key not in codes:
+                    codes[key] = (
+                        keep.tile([P, 512], U32, name="x_codes%d_%d" % key[1:], align_bytes=64),
+                        keep.tile([P, 512], U8, name="x_scales%d_%d" % key[1:], align_bytes=64),
+                    )
+            else:
+                key, cols, fmt = (kind, h, r, s), slice(256 * i, 256 * (i + 1)), E4M3
+                if key not in codes:
+                    codes[key] = (
+                        stream.tile([P, 512], U32, name="w_codes", tag="w_codes", bufs=W_CODE_BUFS, align_bytes=64),
+                        stream.tile([P, 512], U8, name="w_scales", tag="w_scales", bufs=W_CODE_BUFS, align_bytes=64),
+                    )
+            src = grouped[(kind, h, r, i, s)][:].rearrange("p q c u -> p (q c u)").bitcast(BF16)
+            nc.vector.quantize_mx(out=codes[key][0][:, cols].bitcast(fmt), scales=codes[key][1][:, cols], in_=src)
+
+        def multiply(h, r, j, g):
+            first, last = (r, g) == (0, 0), (r, g) == (RANKS - 1, PASSES - 1)
+            if first:
+                acc[(h, j)] = psum.tile([P, N_HALF], F32, name="acc%d" % j, tag="acc%d" % j)
+            x_codes, x_scales = codes[("x", r, j)]
+            w_codes, w_scales = codes[("w", h, r, g)]
+            cols = slice(P * g, P * (g + 1))
+            nc.tensor.matmul_mx(
+                out=acc[(h, j)][:],
+                lhsT=x_codes[:, cols].bitcast(E5M2),
+                lhsT_scale=x_scales[:, cols],
+                rhs=w_codes[:].bitcast(E4M3),
+                rhs_scale=w_scales[:],
+                start=first,
+                stop=last,
+            )
+
+        def bias_part(r, h, j):
+            return bias_sb[r][:, j, N_HALF * h : N_HALF * (h + 1)]
+
+        def empty_acc(h, j):
+            other = bias_part(0, 0, j) if h == 0 else result[(h, j)][:]
+            nc.vector.tensor_tensor(
+                out=result[(h, j)][:].rearrange("m (a p i) -> m a p i", a=2, i=2),
+                in0=acc[(h, j)][:].rearrange("m (a i p) -> m a p i", a=2, i=2),
+                in1=other.rearrange("m (a p i) -> m a p i", a=2, i=2),
+                op=ADD,
+            )
+            if h == 1:
+                store(h, j)
+
+        def add_bias(r, h, j):
+            so_far = bias_part(0, 1, j) if (h, r) == (1, 1) else result[(h, j)][:]
+            nc.vector.tensor_tensor(out=result[(h, j)][:], in0=so_far, in1=bias_part(r, h, j), op=ADD)
+            if (h, r) == (0, RANKS - 1):
+                store(h, j)
+
+        def store(h, j):
+            nc.sync.dma_start(out=out_rows[:, j, N_HALF * h : N_HALF * (h + 1)], in_=result[(h, j)][:])
+
+        rounds = []
+        for kind, h, r, a in first_sweep_pairs:
+            if kind == "x":
+                rounds.append([(kind, h, r, 2 * a + q, s) for q in range(2) for s in range(2)])
+            else:
+                rounds.append([(kind, h, r, a, g) for g in range(PASSES)])
+        sweep2 = len(rounds)
+        for r in range(RANKS):
+            rounds.append([("w", 1, r, a, g) for a in range(2) for g in (0, 1)])
+            rounds.append([("w", 1, r, a, g) for g in (2, 3) for a in range(2)])
+        n_rounds = len(rounds)
+
+        reorders = {k: [] for k in range(-1, n_rounds)}
+        for k, (kind, h, r, a) in enumerate(first_sweep_pairs):
+            reorders[k - 1] = [((kind, h, r, 2 * a + q), False) for q in range(2)]
+        reorders[sweep2 - 1] = [(("w", 1, 0, j), j == 3) for j in range(TILES)]
+        for r in range(1, RANKS):
+            for j in range(TILES):
+                reorders[sweep2 + 2 * (r - 1) + j // 2].append((("w", 1, r, j), j % 2 == 1))
+
+        matmuls = {k: [] for k in range(n_rounds)}
+        for r in range(RANKS):
+            for j in range(TILES):
+                k = 3 + TILES * r + j if r + 1 < RANKS else sweep2 - 1 + j // 2
+                if r == 0:
+                    k = HEAD[j]
+                matmuls[k].extend((0, r, j, g) for g in range(PASSES))
+        for step in range(2 * RANKS - 2):
+            r, gp = divmod(step, 2)
+            matmuls[sweep2 + step + 1].extend((1, r, j, 2 * gp + g2) for j in range(TILES) for g2 in range(2))
+        last = RANKS - 1
+        tail = [(1, last, j, g) for j in range(TILES - 1) for g in (0, 1)]
+        tail.extend((1, last, j, g) for j in range(TILES - 1) for g in (2, 3))
+        tail.extend((1, last, TILES - 1, g) for g in range(PASSES))
+
+        sums = [(empty_acc, (0, 0)), (empty_acc, (0, 1)), (add_bias, (1, 1, 0)), (add_bias, (1, 1, 1))]
+        sums.extend([(empty_acc, (0, 2)), (empty_acc, (0, 3)), (add_bias, (1, 1, 2)), (add_bias, (1, 1, 3))])
+        sums.extend((add_bias, (1, 0, j)) for j in range(TILES))
+        for r in range(2, RANKS):
+            for h in range(2):
+                sums.extend((add_bias, (r, h, j)) for j in range(TILES))
+
+        issue_loads()
+        for tile, on_scalar in reorders[-1]:
+            reorder(tile, on_scalar)
+        for k in range(n_rounds):
+            todo = sums[4 * (k - sweep2) : 4 * (k - sweep2 + 1)] if k >= sweep2 else []
+            for fn, args in todo[:2]:
+                fn(*args)
+            if k >= QFIRST:
+                for tile, on_scalar in reorders[k]:
+                    if not on_scalar:
+                        reorder(tile, False)
+            for i, bank in enumerate(rounds[k]):
+                transpose_bank(*bank)
+                quantize(*bank)
+                if i == 1:
+                    for fn, args in todo[2:]:
+                        fn(*args)
+            for tile, on_scalar in reorders[k]:
+                if on_scalar or k < QFIRST:
+                    reorder(tile, on_scalar)
+            for args in matmuls[k]:
+                multiply(*args)
+        for args in tail:
+            multiply(*args)
+            if args[3] == PASSES - 1:
+                empty_acc(1, args[2])

@@ -18,20 +18,22 @@ P = 128
 TILES = 4
 PASSES = K // 512
 WORDS = K // 2
-N_HALF = N // 2
+N_SWEEP = N // 2
+LAST_RANK = RANKS - 1
 
+TRANSPOSE_BANKS = 4
 RAW_BUFS = 6
-STAGED_BUFS = 8
-GROUPED_BUFS = 12
-W_CODE_BUFS = 10
-HEAD = (3, 4, 5, 6)
-QFIRST = 0
+STAGED_BUFS = 2 * TILES
+GROUPED_BUFS = 3 * TRANSPOSE_BANKS
+W_CODE_BUFS = 2 * PASSES + 2
+SPLIT_PAIRS = 2 * TILES // 2
+SUMS_PER_ROUND = 4
 
 
 def tile_gemmrstritonpcie_kernel(tc, x, weight, bias, out):
     nc = tc.nc
     x_rows = x.rearrange("r (p j) k -> r p j k", j=TILES)
-    w_rows = weight.rearrange("r (h a p j) k -> r h a p j k", h=2, a=2, j=2)
+    w_rows = weight.rearrange("r (h a p i) k -> r h a p i k", h=2, a=2, i=2)
     bias_rows = bias.rearrange("r (p j) n -> r p j n", j=TILES)
     out_rows = out.rearrange("r m n -> (r m) n").rearrange("(p j) n -> p j n", j=TILES)
 
@@ -45,94 +47,89 @@ def tile_gemmrstritonpcie_kernel(tc, x, weight, bias, out):
         make_identity(nc, ident[:])
         bias_sb = [keep.tile([P, TILES, N], BF16, name="bias%d" % r) for r in range(RANKS)]
         result = {
-            (h, j): keep.tile([P, N_HALF], F32, name="result%d_%d" % (h, j))
+            (h, j): keep.tile([P, N_SWEEP], F32, name="result%d_%d" % (h, j))
             for h in range(2)
             for j in range(TILES)
         }
-
         raw, staged, grouped, codes, acc = {}, {}, {}, {}, {}
 
-        loads = [("w", 0, 0, 0), ("w", 0, 0, 1)]
+        sweep0_pairs = [("w", 0, 0, a) for a in range(2)]
         for r in range(RANKS):
-            for a in range(2):
-                loads.append(("x", 0, r, a))
-                if r + 1 < RANKS:
-                    loads.append(("w", 0, r + 1, a))
-        first_sweep_pairs = list(loads)
-        loads.extend([("w", 1, 0, 0), ("w", 1, 0, 1), ("bias", 0)])
+            sweep0_pairs.extend(("x", 0, r, a) for a in range(2))
+            if r < LAST_RANK:
+                sweep0_pairs.extend(("w", 0, r + 1, a) for a in range(2))
+        loads = sweep0_pairs + [("w", 1, 0, 0), ("w", 1, 0, 1), ("bias", 0)]
         for r in range(1, RANKS):
             loads.extend([("w", 1, r, 0), ("bias", r), ("w", 1, r, 1)])
-        split_pairs = 3
-        state = {"load": 0, "pairs": 0, "reordered": 0}
 
         def issue_loads():
-            while state["load"] < len(loads):
-                item = loads[state["load"]]
-                if item[0] == "bias":
-                    nc.sync.dma_start(out=bias_sb[item[1]][:], in_=bias_rows[item[1]])
+            while loads:
+                if loads[0][0] == "bias":
+                    r = loads[0][1]
+                    nc.sync.dma_start(out=bias_sb[r][:], in_=bias_rows[r])
                 else:
-                    if state["pairs"] - RAW_BUFS >= state["reordered"] // 2:
+                    pairs_loaded = len(raw) // 2
+                    if pairs_loaded - RAW_BUFS >= len(staged) // 2:
                         return
-                    kind, h, r, a = item
-                    src = x_rows[r, :, 2 * a : 2 * a + 2, :] if kind == "x" else w_rows[r, h, a]
+                    operand, h, r, a = loads[0]
+                    src = x_rows[r, :, 2 * a : 2 * a + 2, :] if operand == "x" else w_rows[r, h, a]
                     pair = stream.tile([P, 2, K], BF16, name="raw", tag="raw", bufs=RAW_BUFS)
-                    if state["pairs"] < split_pairs:
-                        for jj in range(2):
-                            nc.sync.dma_start(out=pair[:, jj, :], in_=src[:, jj, :])
+                    if pairs_loaded < SPLIT_PAIRS:
+                        for i in range(2):
+                            nc.sync.dma_start(out=pair[:, i, :], in_=src[:, i, :])
                     else:
                         nc.sync.dma_start(out=pair[:], in_=src)
-                    for jj in range(2):
-                        raw[(kind, h, r, 2 * a + jj)] = pair[:, jj, :]
-                    state["pairs"] += 1
-                state["load"] += 1
+                    for i in range(2):
+                        raw[(operand, h, r, 2 * a + i)] = pair[:, i, :]
+                loads.pop(0)
 
-        def reorder(tile, on_scalar):
-            dst = stream.tile([P, 2, WORDS // 2], F32, name="staged", tag="staged", bufs=STAGED_BUFS)
-            src = raw[tile].bitcast(F32).rearrange("p (b u e) -> p u b e", u=2, e=8)
-            view = dst[:].rearrange("p u (b e) -> p u b e", e=8)
-            if on_scalar:
-                nc.scalar.copy(out=view, in_=src)
-            else:
-                nc.vector.tensor_copy(out=view, in_=src)
-            staged[tile] = dst
-            state["reordered"] += 1
+        def reorder(tile, copy):
+            staged[tile] = stream.tile([P, 2, WORDS // 2], F32, name="staged", tag="staged", bufs=STAGED_BUFS)
+            copy(
+                out=staged[tile][:].rearrange("p u (b e) -> p u b e", e=8),
+                in_=raw[tile].bitcast(F32).rearrange("p (b u e) -> p u b e", u=2, e=8),
+            )
             issue_loads()
 
-        def transpose_bank(kind, h, r, i, s):
-            if kind == "x":
-                parts = [((kind, h, r, i), 2 * s + q) for q in range(2)]
+        def transpose_bank(operand, h, r, i, s):
+            if operand == "x":
+                parts = [((operand, h, r, i), 2 * s + q) for q in range(2)]
             else:
-                parts = [((kind, h, r, 2 * i + q), s) for q in range(2)]
-            bank = psum.tile([P, 2, 2, P], F32, name="bank", tag="bank", bufs=4)
+                parts = [((operand, h, r, 2 * i + q), s) for q in range(2)]
+            bank = psum.tile([P, 2, 2, P], F32, name="bank", tag="bank", bufs=TRANSPOSE_BANKS)
             for q, (tile, g) in enumerate(parts):
                 for u in range(2):
                     nc.tensor.transpose(bank[:, q, u, :], staged[tile][:, u, P * g : P * (g + 1)], ident[:])
-            dst = stream.tile([P, 2, P, 2], F32, name="grouped", tag="grouped", bufs=GROUPED_BUFS, align_bytes=64)
-            nc.scalar.copy(out=dst[:], in_=bank[:].rearrange("p q u c -> p q c u"))
-            grouped[(kind, h, r, i, s)] = dst
+            words = stream.tile([P, 2, P, 2], F32, name="grouped", tag="grouped", bufs=GROUPED_BUFS, align_bytes=64)
+            nc.scalar.copy(out=words[:], in_=bank[:].rearrange("p q u row -> p q row u"))
+            grouped[(operand, h, r, i, s)] = words
 
-        def quantize(kind, h, r, i, s):
-            if kind == "x":
-                key, cols, fmt = (kind, r, i), slice(256 * s, 256 * (s + 1)), E5M2
+        def quantize(operand, h, r, i, s):
+            if operand == "x":
+                key, part, fmt = (operand, r, i), s, E5M2
                 if key not in codes:
                     codes[key] = (
-                        keep.tile([P, 512], U32, name="x_codes%d_%d" % key[1:], align_bytes=64),
-                        keep.tile([P, 512], U8, name="x_scales%d_%d" % key[1:], align_bytes=64),
+                        keep.tile([P, PASSES * P], U32, name="x_codes%d_%d" % (r, i), align_bytes=64),
+                        keep.tile([P, PASSES * P], U8, name="x_scales%d_%d" % (r, i), align_bytes=64),
                     )
             else:
-                key, cols, fmt = (kind, h, r, s), slice(256 * i, 256 * (i + 1)), E4M3
+                key, part, fmt = (operand, h, r, s), i, E4M3
                 if key not in codes:
                     codes[key] = (
-                        stream.tile([P, 512], U32, name="w_codes", tag="w_codes", bufs=W_CODE_BUFS, align_bytes=64),
-                        stream.tile([P, 512], U8, name="w_scales", tag="w_scales", bufs=W_CODE_BUFS, align_bytes=64),
+                        stream.tile([P, N_SWEEP], U32, name="w_codes", tag="w_codes", bufs=W_CODE_BUFS, align_bytes=64),
+                        stream.tile([P, N_SWEEP], U8, name="w_scales", tag="w_scales", bufs=W_CODE_BUFS, align_bytes=64),
                     )
-            src = grouped[(kind, h, r, i, s)][:].rearrange("p q c u -> p (q c u)").bitcast(BF16)
-            nc.vector.quantize_mx(out=codes[key][0][:, cols].bitcast(fmt), scales=codes[key][1][:, cols], in_=src)
+            cols = slice(2 * P * part, 2 * P * (part + 1))
+            nc.vector.quantize_mx(
+                out=codes[key][0][:, cols].bitcast(fmt),
+                scales=codes[key][1][:, cols],
+                in_=grouped[(operand, h, r, i, s)][:].rearrange("p q row u -> p (q row u)").bitcast(BF16),
+            )
 
         def multiply(h, r, j, g):
-            first, last = (r, g) == (0, 0), (r, g) == (RANKS - 1, PASSES - 1)
+            first, last = (r, g) == (0, 0), (r, g) == (LAST_RANK, PASSES - 1)
             if first:
-                acc[(h, j)] = psum.tile([P, N_HALF], F32, name="acc%d" % j, tag="acc%d" % j)
+                acc[(h, j)] = psum.tile([P, N_SWEEP], F32, name="acc%d" % j, tag="acc%d" % j)
             x_codes, x_scales = codes[("x", r, j)]
             w_codes, w_scales = codes[("w", h, r, g)]
             cols = slice(P * g, P * (g + 1))
@@ -147,93 +144,95 @@ def tile_gemmrstritonpcie_kernel(tc, x, weight, bias, out):
             )
 
         def bias_part(r, h, j):
-            return bias_sb[r][:, j, N_HALF * h : N_HALF * (h + 1)]
+            return bias_sb[r][:, j, N_SWEEP * h : N_SWEEP * (h + 1)]
 
-        def empty_acc(h, j):
-            other = bias_part(0, 0, j) if h == 0 else result[(h, j)][:]
+        def store(h, j, cols):
+            nc.sync.dma_start(out=out_rows[:, j, N_SWEEP * h : N_SWEEP * (h + 1)][:, cols], in_=result[(h, j)][:, cols])
+
+        def empty_acc(h, j, cols):
+            addend = bias_part(0, 0, j) if h == 0 else result[(h, j)][:]
             nc.vector.tensor_tensor(
-                out=result[(h, j)][:].rearrange("m (a p i) -> m a p i", a=2, i=2),
-                in0=acc[(h, j)][:].rearrange("m (a i p) -> m a p i", a=2, i=2),
-                in1=other.rearrange("m (a p i) -> m a p i", a=2, i=2),
+                out=result[(h, j)][:, cols].rearrange("m (a c i) -> m a c i", c=P, i=2),
+                in0=acc[(h, j)][:, cols].rearrange("m (a i c) -> m a c i", c=P, i=2),
+                in1=addend[:, cols].rearrange("m (a c i) -> m a c i", c=P, i=2),
                 op=ADD,
             )
             if h == 1:
-                store(h, j)
+                store(h, j, cols)
 
         def add_bias(r, h, j):
             so_far = bias_part(0, 1, j) if (h, r) == (1, 1) else result[(h, j)][:]
             nc.vector.tensor_tensor(out=result[(h, j)][:], in0=so_far, in1=bias_part(r, h, j), op=ADD)
-            if (h, r) == (0, RANKS - 1):
-                store(h, j)
-
-        def store(h, j):
-            nc.sync.dma_start(out=out_rows[:, j, N_HALF * h : N_HALF * (h + 1)], in_=result[(h, j)][:])
+            if (h, r) == (0, LAST_RANK):
+                store(h, j, slice(0, N_SWEEP))
 
         rounds = []
-        for kind, h, r, a in first_sweep_pairs:
-            if kind == "x":
-                rounds.append([(kind, h, r, 2 * a + q, s) for q in range(2) for s in range(2)])
+        for operand, h, r, a in sweep0_pairs:
+            if operand == "x":
+                rounds.append([(operand, h, r, 2 * a + q, s) for q in range(2) for s in range(2)])
             else:
-                rounds.append([(kind, h, r, a, g) for g in range(PASSES)])
-        sweep2 = len(rounds)
+                rounds.append([(operand, h, r, a, g) for g in range(PASSES)])
+        sweep1 = len(rounds)
         for r in range(RANKS):
             rounds.append([("w", 1, r, a, g) for a in range(2) for g in (0, 1)])
             rounds.append([("w", 1, r, a, g) for g in (2, 3) for a in range(2)])
-        n_rounds = len(rounds)
+        last_round = len(rounds) - 1
 
-        reorders = {k: [] for k in range(-1, n_rounds)}
-        for k, (kind, h, r, a) in enumerate(first_sweep_pairs):
-            reorders[k - 1] = [((kind, h, r, 2 * a + q), False) for q in range(2)]
-        reorders[sweep2 - 1] = [(("w", 1, 0, j), j == 3) for j in range(TILES)]
+        on_vector = {k: [] for k in range(-1, last_round + 1)}
+        on_scalar = {k: [] for k in range(-1, last_round + 1)}
+        for k, (operand, h, r, a) in enumerate(sweep0_pairs):
+            on_vector[k - 1] = [(operand, h, r, 2 * a + q) for q in range(2)]
+        on_vector[sweep1 - 1] = [("w", 1, 0, j) for j in range(TILES - 1)]
+        on_scalar[sweep1 - 1] = [("w", 1, 0, TILES - 1)]
         for r in range(1, RANKS):
-            for j in range(TILES):
-                reorders[sweep2 + 2 * (r - 1) + j // 2].append((("w", 1, r, j), j % 2 == 1))
+            for a in range(2):
+                on_vector[sweep1 + 2 * (r - 1) + a] = [("w", 1, r, 2 * a)]
+                on_scalar[sweep1 + 2 * (r - 1) + a] = [("w", 1, r, 2 * a + 1)]
 
-        matmuls = {k: [] for k in range(n_rounds)}
+        matmuls = {k: [] for k in range(last_round + 1)}
         for r in range(RANKS):
+            after_x = sweep0_pairs.index(("x", 0, r, 0)) + 1
             for j in range(TILES):
-                k = 3 + TILES * r + j if r + 1 < RANKS else sweep2 - 1 + j // 2
-                if r == 0:
-                    k = HEAD[j]
+                k = after_x + (j if r < LAST_RANK else j // 2)
                 matmuls[k].extend((0, r, j, g) for g in range(PASSES))
-        for step in range(2 * RANKS - 2):
-            r, gp = divmod(step, 2)
-            matmuls[sweep2 + step + 1].extend((1, r, j, 2 * gp + g2) for j in range(TILES) for g2 in range(2))
-        last = RANKS - 1
-        tail = [(1, last, j, g) for j in range(TILES - 1) for g in (0, 1)]
-        tail.extend((1, last, j, g) for j in range(TILES - 1) for g in (2, 3))
-        tail.extend((1, last, TILES - 1, g) for g in range(PASSES))
+        for step in range(2 * LAST_RANK):
+            r, s = divmod(step, 2)
+            matmuls[sweep1 + step + 1].extend((1, r, j, 2 * s + q) for j in range(TILES) for q in range(2))
+        tail = [(1, LAST_RANK, j, g) for s in range(2) for j in range(TILES - 1) for g in (2 * s, 2 * s + 1)]
+        tail.extend((1, LAST_RANK, TILES - 1, g) for g in range(PASSES))
 
-        sums = [(empty_acc, (0, 0)), (empty_acc, (0, 1)), (add_bias, (1, 1, 0)), (add_bias, (1, 1, 1))]
-        sums.extend([(empty_acc, (0, 2)), (empty_acc, (0, 3)), (add_bias, (1, 1, 2)), (add_bias, (1, 1, 3))])
+        sums = []
+        for a in range(2):
+            sums.extend((empty_acc, (0, j, slice(0, N_SWEEP))) for j in (2 * a, 2 * a + 1))
+            sums.extend((add_bias, (1, 1, j)) for j in (2 * a, 2 * a + 1))
         sums.extend((add_bias, (1, 0, j)) for j in range(TILES))
         for r in range(2, RANKS):
-            for h in range(2):
-                sums.extend((add_bias, (r, h, j)) for j in range(TILES))
+            sums.extend((add_bias, (r, h, j)) for h in range(2) for j in range(TILES))
 
         issue_loads()
-        for tile, on_scalar in reorders[-1]:
-            reorder(tile, on_scalar)
-        for k in range(n_rounds):
-            todo = sums[4 * (k - sweep2) : 4 * (k - sweep2 + 1)] if k >= sweep2 else []
-            for fn, args in todo[:2]:
-                fn(*args)
-            if k >= QFIRST:
-                for tile, on_scalar in reorders[k]:
-                    if not on_scalar:
-                        reorder(tile, False)
-            for i, bank in enumerate(rounds[k]):
-                transpose_bank(*bank)
-                quantize(*bank)
-                if i == 1:
-                    for fn, args in todo[2:]:
-                        fn(*args)
-            for tile, on_scalar in reorders[k]:
-                if on_scalar or k < QFIRST:
-                    reorder(tile, on_scalar)
+        for tile in on_vector[-1]:
+            reorder(tile, nc.vector.tensor_copy)
+        for k, banks in enumerate(rounds):
+            for bank_name in banks:
+                transpose_bank(*bank_name)
+            due = sums[SUMS_PER_ROUND * (k - sweep1) : SUMS_PER_ROUND * (k - sweep1 + 1)] if k >= sweep1 else []
+            for bank_name in rounds[k - 1][2:] if k > 0 else []:
+                quantize(*bank_name)
+            for tile in on_vector[k]:
+                reorder(tile, nc.vector.tensor_copy)
+            for addition, args in due[: SUMS_PER_ROUND // 2]:
+                addition(*args)
+            for bank_name in banks if k == last_round else banks[:2]:
+                quantize(*bank_name)
+            for addition, args in due[SUMS_PER_ROUND // 2 :]:
+                addition(*args)
+            for tile in on_scalar[k]:
+                reorder(tile, nc.scalar.copy)
             for args in matmuls[k]:
                 multiply(*args)
-        for args in tail:
-            multiply(*args)
-            if args[3] == PASSES - 1:
-                empty_acc(1, args[2])
+        for h, r, j, g in tail:
+            multiply(h, r, j, g)
+            if g == PASSES - 1 and j < TILES - 1:
+                empty_acc(h, j, slice(0, N_SWEEP))
+        for a in range(2):
+            empty_acc(1, TILES - 1, slice(2 * P * a, 2 * P * (a + 1)))

@@ -22,12 +22,12 @@ N_SWEEP = N // 2
 LAST_RANK = RANKS - 1
 
 TRANSPOSE_BANKS = 4
-RAW_BUFS = 6
-STAGED_BUFS = 2 * TILES
+RAW_BUFS = 7
+STAGED_BUFS = 6
 GROUPED_BUFS = 3 * TRANSPOSE_BANKS
-W_CODE_BUFS = 2 * PASSES + 2
-SPLIT_PAIRS = 2 * TILES // 2
-SUMS_PER_ROUND = 4
+W_CODE_BUFS = 3 * PASSES
+SPLIT_PAIRS = 4
+ADDITIONS_PER_ROUND = 4
 
 
 def tile_gemmrstritonpcie_kernel(tc, x, weight, bias, out):
@@ -53,13 +53,15 @@ def tile_gemmrstritonpcie_kernel(tc, x, weight, bias, out):
         }
         raw, staged, grouped, codes, acc = {}, {}, {}, {}, {}
 
-        sweep0_pairs = [("w", 0, 0, a) for a in range(2)]
+        pairs = [("w", 0, 0, a) for a in range(2)]
         for r in range(RANKS):
-            sweep0_pairs.extend(("x", 0, r, a) for a in range(2))
+            pairs.extend(("x", 0, r, a) for a in range(2))
             if r < LAST_RANK:
-                sweep0_pairs.extend(("w", 0, r + 1, a) for a in range(2))
-        loads = sweep0_pairs + [("w", 1, 0, 0), ("w", 1, 0, 1), ("bias", 0)]
-        for r in range(1, RANKS):
+                pairs.extend(("w", 0, r + 1, a) for a in range(2))
+        sweep1 = len(pairs)
+        loads = list(pairs)
+        for r in range(RANKS):
+            pairs.extend(("w", 1, r, a) for a in range(2))
             loads.extend([("w", 1, r, 0), ("bias", r), ("w", 1, r, 1)])
 
         def issue_loads():
@@ -167,67 +169,68 @@ def tile_gemmrstritonpcie_kernel(tc, x, weight, bias, out):
                 store(h, j, slice(0, N_SWEEP))
 
         rounds = []
-        for operand, h, r, a in sweep0_pairs:
+        for operand, h, r, a in pairs:
             if operand == "x":
                 rounds.append([(operand, h, r, 2 * a + q, s) for q in range(2) for s in range(2)])
             else:
                 rounds.append([(operand, h, r, a, g) for g in range(PASSES)])
-        sweep1 = len(rounds)
-        for r in range(RANKS):
-            rounds.append([("w", 1, r, a, g) for a in range(2) for g in (0, 1)])
-            rounds.append([("w", 1, r, a, g) for g in (2, 3) for a in range(2)])
         last_round = len(rounds) - 1
 
-        on_vector = {k: [] for k in range(-1, last_round + 1)}
-        on_scalar = {k: [] for k in range(-1, last_round + 1)}
-        for k, (operand, h, r, a) in enumerate(sweep0_pairs):
-            on_vector[k - 1] = [(operand, h, r, 2 * a + q) for q in range(2)]
-        on_vector[sweep1 - 1] = [("w", 1, 0, j) for j in range(TILES - 1)]
-        on_scalar[sweep1 - 1] = [("w", 1, 0, TILES - 1)]
-        for r in range(1, RANKS):
-            for a in range(2):
-                on_vector[sweep1 + 2 * (r - 1) + a] = [("w", 1, r, 2 * a)]
-                on_scalar[sweep1 + 2 * (r - 1) + a] = [("w", 1, r, 2 * a + 1)]
-
         matmuls = {k: [] for k in range(last_round + 1)}
+        closed = {k: [] for k in range(last_round + 1)}
         for r in range(RANKS):
-            after_x = sweep0_pairs.index(("x", 0, r, 0)) + 1
+            after_x = pairs.index(("x", 0, r, 0)) + 1
             for j in range(TILES):
-                k = after_x + (j if r < LAST_RANK else j // 2)
+                k = min(after_x + j, sweep1 + 1)
                 matmuls[k].extend((0, r, j, g) for g in range(PASSES))
-        for step in range(2 * LAST_RANK):
-            r, s = divmod(step, 2)
-            matmuls[sweep1 + step + 1].extend((1, r, j, 2 * s + q) for j in range(TILES) for q in range(2))
-        tail = [(1, LAST_RANK, j, g) for s in range(2) for j in range(TILES - 1) for g in (2 * s, 2 * s + 1)]
-        tail.extend((1, LAST_RANK, TILES - 1, g) for g in range(PASSES))
+                if r == LAST_RANK:
+                    closed[k + 1].append(j)
+        for r in range(LAST_RANK):
+            for s in range(2):
+                k = pairs.index(("w", 1, r + 1, s))
+                matmuls[k].extend((1, r, j, 2 * s + q) for j in range(TILES) for q in range(2))
+        tail = [(1, LAST_RANK, j, g) for j in range(TILES) for g in range(PASSES)]
 
-        sums = []
-        for a in range(2):
-            sums.extend((empty_acc, (0, j, slice(0, N_SWEEP))) for j in (2 * a, 2 * a + 1))
-            sums.extend((add_bias, (1, 1, j)) for j in (2 * a, 2 * a + 1))
-        sums.extend((add_bias, (1, 0, j)) for j in range(TILES))
-        for r in range(2, RANKS):
-            sums.extend((add_bias, (r, h, j)) for h in range(2) for j in range(TILES))
+        bias_additions = [(1, h, j) for h in (1, 0) for j in range(TILES)]
+        bias_additions.extend((r, h, j) for r in range(2, RANKS) for h in range(2) for j in range(TILES))
+        first_bias_round = sweep1 + 1
+
+        def add_biases(count):
+            for args in bias_additions[:count]:
+                add_bias(*args)
+                bias_additions.remove(args)
 
         issue_loads()
-        for tile in on_vector[-1]:
-            reorder(tile, nc.vector.tensor_copy)
+        for i in range(2):
+            reorder(("w", 0, 0, i), nc.vector.tensor_copy)
         for k, banks in enumerate(rounds):
-            for bank_name in banks:
+            next_tiles = []
+            if k < last_round:
+                operand, h, r, a = pairs[k + 1]
+                next_tiles = [(operand, h, r, 2 * a + i) for i in range(2)]
+            vector_share = 2 if k < first_bias_round else 1
+            for bank_name in banks[:2]:
                 transpose_bank(*bank_name)
-            due = sums[SUMS_PER_ROUND * (k - sweep1) : SUMS_PER_ROUND * (k - sweep1 + 1)] if k >= sweep1 else []
+            for tile in next_tiles[vector_share:]:
+                reorder(tile, nc.scalar.copy)
+            for bank_name in banks[2:]:
+                transpose_bank(*bank_name)
+
             for bank_name in rounds[k - 1][2:] if k > 0 else []:
                 quantize(*bank_name)
-            for tile in on_vector[k]:
+            for tile in next_tiles[:vector_share]:
                 reorder(tile, nc.vector.tensor_copy)
-            for addition, args in due[: SUMS_PER_ROUND // 2]:
-                addition(*args)
+            for j in closed[k]:
+                empty_acc(0, j, slice(0, N_SWEEP))
+            if k >= first_bias_round and not closed[k]:
+                add_biases(ADDITIONS_PER_ROUND // 2)
             for bank_name in banks if k == last_round else banks[:2]:
                 quantize(*bank_name)
-            for addition, args in due[SUMS_PER_ROUND // 2 :]:
-                addition(*args)
-            for tile in on_scalar[k]:
-                reorder(tile, nc.scalar.copy)
+            if k == last_round:
+                add_biases(len(bias_additions))
+            elif k >= first_bias_round:
+                add_biases(ADDITIONS_PER_ROUND - 1 - len(closed[k]) if closed[k] else ADDITIONS_PER_ROUND // 2)
+
             for args in matmuls[k]:
                 multiply(*args)
         for h, r, j, g in tail:

from contextlib import ExitStack

import concourse.mybir as mybir
from concourse.masks import make_identity

RANKS, M, K, N = 4, 512, 2048, 1024
FLOPS = 2 * RANKS * M * K * N

F32 = mybir.dt.float32
BF16 = mybir.dt.bfloat16
U32 = mybir.dt.uint32
U8 = mybir.dt.uint8
E5M2 = mybir.dt.float8_e5m2_x4
E4M3 = mybir.dt.float8_e4m3fn_x4
ADD = mybir.AluOpType.add

P = 128
TILES = 4
PASSES = K // 512
WORDS = K // 2
N_SWEEP = N // 2
LAST_RANK = RANKS - 1

TRANSPOSE_BANKS = 4
RAW_BUFS = 7
STAGED_BUFS = 6
GROUPED_BUFS = 3 * TRANSPOSE_BANKS
W_CODE_BUFS = 3 * PASSES
SPLIT_PAIRS = 4
ADDITIONS_PER_ROUND = 4


def tile_gemmrstritonpcie_kernel(tc, x, weight, bias, out):
    nc = tc.nc
    x_rows = x.rearrange("r (p j) k -> r p j k", j=TILES)
    w_rows = weight.rearrange("r (h a p i) k -> r h a p i k", h=2, a=2, i=2)
    bias_rows = bias.rearrange("r (p j) n -> r p j n", j=TILES)
    out_rows = out.rearrange("r m n -> (r m) n").rearrange("(p j) n -> p j n", j=TILES)

    with ExitStack() as ctx:
        keep = ctx.enter_context(tc.tile_pool(name="keep", bufs=1))
        stream = ctx.enter_context(tc.tile_pool(name="stream", bufs=1))
        psum = ctx.enter_context(tc.psum_pool(name="psum", bufs=1))
        ctx.enter_context(tc.manual_schedule())

        ident = keep.tile([P, P], F32, name="ident")
        make_identity(nc, ident[:])
        bias_sb = [keep.tile([P, TILES, N], BF16, name="bias%d" % r) for r in range(RANKS)]
        result = {
            (h, j): keep.tile([P, N_SWEEP], F32, name="result%d_%d" % (h, j))
            for h in range(2)
            for j in range(TILES)
        }
        raw, staged, grouped, codes, acc = {}, {}, {}, {}, {}

        pairs = [("w", 0, 0, a) for a in range(2)]
        for r in range(RANKS):
            pairs.extend(("x", 0, r, a) for a in range(2))
            if r < LAST_RANK:
                pairs.extend(("w", 0, r + 1, a) for a in range(2))
        sweep1 = len(pairs)
        loads = list(pairs)
        for r in range(RANKS):
            pairs.extend(("w", 1, r, a) for a in range(2))
            loads.extend([("w", 1, r, 0), ("bias", r), ("w", 1, r, 1)])

        def issue_loads():
            while loads:
                if loads[0][0] == "bias":
                    r = loads[0][1]
                    nc.sync.dma_start(out=bias_sb[r][:], in_=bias_rows[r])
                else:
                    pairs_loaded = len(raw) // 2
                    if pairs_loaded - RAW_BUFS >= len(staged) // 2:
                        return
                    operand, h, r, a = loads[0]
                    src = x_rows[r, :, 2 * a : 2 * a + 2, :] if operand == "x" else w_rows[r, h, a]
                    pair = stream.tile([P, 2, K], BF16, name="raw", tag="raw", bufs=RAW_BUFS)
                    if pairs_loaded < SPLIT_PAIRS:
                        for i in range(2):
                            nc.sync.dma_start(out=pair[:, i, :], in_=src[:, i, :])
                    else:
                        nc.sync.dma_start(out=pair[:], in_=src)
                    for i in range(2):
                        raw[(operand, h, r, 2 * a + i)] = pair[:, i, :]
                loads.pop(0)

        def reorder(tile, copy):
            staged[tile] = stream.tile([P, 2, WORDS // 2], F32, name="staged", tag="staged", bufs=STAGED_BUFS)
            copy(
                out=staged[tile][:].rearrange("p u (b e) -> p u b e", e=8),
                in_=raw[tile].bitcast(F32).rearrange("p (b u e) -> p u b e", u=2, e=8),
            )
            issue_loads()

        def transpose_bank(operand, h, r, i, s):
            if operand == "x":
                parts = [((operand, h, r, i), 2 * s + q) for q in range(2)]
            else:
                parts = [((operand, h, r, 2 * i + q), s) for q in range(2)]
            bank = psum.tile([P, 2, 2, P], F32, name="bank", tag="bank", bufs=TRANSPOSE_BANKS)
            for q, (tile, g) in enumerate(parts):
                for u in range(2):
                    nc.tensor.transpose(bank[:, q, u, :], staged[tile][:, u, P * g : P * (g + 1)], ident[:])
            words = stream.tile([P, 2, P, 2], F32, name="grouped", tag="grouped", bufs=GROUPED_BUFS, align_bytes=64)
            nc.scalar.copy(out=words[:], in_=bank[:].rearrange("p q u row -> p q row u"))
            grouped[(operand, h, r, i, s)] = words

        def quantize(operand, h, r, i, s):
            if operand == "x":
                key, part, fmt = (operand, r, i), s, E5M2
                if key not in codes:
                    codes[key] = (
                        keep.tile([P, PASSES * P], U32, name="x_codes%d_%d" % (r, i), align_bytes=64),
                        keep.tile([P, PASSES * P], U8, name="x_scales%d_%d" % (r, i), align_bytes=64),
                    )
            else:
                key, part, fmt = (operand, h, r, s), i, E4M3
                if key not in codes:
                    codes[key] = (
                        stream.tile([P, N_SWEEP], U32, name="w_codes", tag="w_codes", bufs=W_CODE_BUFS, align_bytes=64),
                        stream.tile([P, N_SWEEP], U8, name="w_scales", tag="w_scales", bufs=W_CODE_BUFS, align_bytes=64),
                    )
            cols = slice(2 * P * part, 2 * P * (part + 1))
            nc.vector.quantize_mx(
                out=codes[key][0][:, cols].bitcast(fmt),
                scales=codes[key][1][:, cols],
                in_=grouped[(operand, h, r, i, s)][:].rearrange("p q row u -> p (q row u)").bitcast(BF16),
            )

        def multiply(h, r, j, g):
            first, last = (r, g) == (0, 0), (r, g) == (LAST_RANK, PASSES - 1)
            if first:
                acc[(h, j)] = psum.tile([P, N_SWEEP], F32, name="acc%d" % j, tag="acc%d" % j)
            x_codes, x_scales = codes[("x", r, j)]
            w_codes, w_scales = codes[("w", h, r, g)]
            cols = slice(P * g, P * (g + 1))
            nc.tensor.matmul_mx(
                out=acc[(h, j)][:],
                lhsT=x_codes[:, cols].bitcast(E5M2),
                lhsT_scale=x_scales[:, cols],
                rhs=w_codes[:].bitcast(E4M3),
                rhs_scale=w_scales[:],
                start=first,
                stop=last,
            )

        def bias_part(r, h, j):
            return bias_sb[r][:, j, N_SWEEP * h : N_SWEEP * (h + 1)]

        def store(h, j, cols):
            nc.sync.dma_start(out=out_rows[:, j, N_SWEEP * h : N_SWEEP * (h + 1)][:, cols], in_=result[(h, j)][:, cols])

        def empty_acc(h, j, cols):
            addend = bias_part(0, 0, j) if h == 0 else result[(h, j)][:]
            nc.vector.tensor_tensor(
                out=result[(h, j)][:, cols].rearrange("m (a c i) -> m a c i", c=P, i=2),
                in0=acc[(h, j)][:, cols].rearrange("m (a i c) -> m a c i", c=P, i=2),
                in1=addend[:, cols].rearrange("m (a c i) -> m a c i", c=P, i=2),
                op=ADD,
            )
            if h == 1:
                store(h, j, cols)

        def add_bias(r, h, j):
            so_far = bias_part(0, 1, j) if (h, r) == (1, 1) else result[(h, j)][:]
            nc.vector.tensor_tensor(out=result[(h, j)][:], in0=so_far, in1=bias_part(r, h, j), op=ADD)
            if (h, r) == (0, LAST_RANK):
                store(h, j, slice(0, N_SWEEP))

        rounds = []
        for operand, h, r, a in pairs:
            if operand == "x":
                rounds.append([(operand, h, r, 2 * a + q, s) for q in range(2) for s in range(2)])
            else:
                rounds.append([(operand, h, r, a, g) for g in range(PASSES)])
        last_round = len(rounds) - 1

        matmuls = {k: [] for k in range(last_round + 1)}
        closed = {k: [] for k in range(last_round + 1)}
        for r in range(RANKS):
            after_x = pairs.index(("x", 0, r, 0)) + 1
            for j in range(TILES):
                k = min(after_x + j, sweep1 + 1)
                matmuls[k].extend((0, r, j, g) for g in range(PASSES))
                if r == LAST_RANK:
                    closed[k + 1].append(j)
        for r in range(LAST_RANK):
            for s in range(2):
                k = pairs.index(("w", 1, r + 1, s))
                matmuls[k].extend((1, r, j, 2 * s + q) for j in range(TILES) for q in range(2))
        tail = [(1, LAST_RANK, j, g) for j in range(TILES) for g in range(PASSES)]

        bias_additions = [(1, h, j) for h in (1, 0) for j in range(TILES)]
        bias_additions.extend((r, h, j) for r in range(2, RANKS) for h in range(2) for j in range(TILES))
        first_bias_round = sweep1 + 1

        def add_biases(count):
            for args in bias_additions[:count]:
                add_bias(*args)
                bias_additions.remove(args)

        issue_loads()
        for i in range(2):
            reorder(("w", 0, 0, i), nc.vector.tensor_copy)
        for k, banks in enumerate(rounds):
            next_tiles = []
            if k < last_round:
                operand, h, r, a = pairs[k + 1]
                next_tiles = [(operand, h, r, 2 * a + i) for i in range(2)]
            vector_share = 2 if k < first_bias_round else 1
            for bank_name in banks[:2]:
                transpose_bank(*bank_name)
            for tile in next_tiles[vector_share:]:
                reorder(tile, nc.scalar.copy)
            for bank_name in banks[2:]:
                transpose_bank(*bank_name)

            for bank_name in rounds[k - 1][2:] if k > 0 else []:
                quantize(*bank_name)
            for tile in next_tiles[:vector_share]:
                reorder(tile, nc.vector.tensor_copy)
            for j in closed[k]:
                empty_acc(0, j, slice(0, N_SWEEP))
            if k >= first_bias_round and not closed[k]:
                add_biases(ADDITIONS_PER_ROUND // 2)
            for bank_name in banks if k == last_round else banks[:2]:
                quantize(*bank_name)
            if k == last_round:
                add_biases(len(bias_additions))
            elif k >= first_bias_round:
                add_biases(ADDITIONS_PER_ROUND - 1 - len(closed[k]) if closed[k] else ADDITIONS_PER_ROUND // 2)

            for args in matmuls[k]:
                multiply(*args)
        for h, r, j, g in tail:
            multiply(h, r, j, g)
            if g == PASSES - 1 and j < TILES - 1:
                empty_acc(h, j, slice(0, N_SWEEP))
        for a in range(2):
            empty_acc(1, TILES - 1, slice(2 * P * a, 2 * P * (a + 1)))
